import numpy as np
import ml_dtypes


def mxq(x, axis, fmt="e4m3"):
    dtype, down = {"e4m3": (ml_dtypes.float8_e4m3fn, 7), "e5m2": (ml_dtypes.float8_e5m2, 14)}[fmt]
    v = np.moveaxis(np.asarray(x, np.float32).astype(ml_dtypes.bfloat16).astype(np.float64), axis, -1)
    blocks = v.reshape(v.shape[:-1] + (-1, 32))
    amax = np.abs(blocks).max(-1, keepdims=True)
    byte = np.maximum(np.where(amax > 0, np.frexp(amax)[1] - 1 + 127, 0) - down, 1)
    scale = np.exp2(byte - 127.0)
    codes = (blocks / scale).astype(np.float32).astype(dtype).astype(np.float64)
    return np.moveaxis((codes * scale).reshape(v.shape), -1, axis)


WIDE = False


def mx_kscale(k):
    if not WIDE:
        return np.ones(k)
    levels = np.array([10, -10, 5, -5, 0])
    if k % 512:
        return np.exp2(np.random.permutation(np.resize(levels, k // 32))).repeat(32)
    a = np.empty((k // 512, 16))
    for p in range(k // 512):
        a[p, :8] = np.random.permutation(np.resize(levels, 8))
        for g in range(8):
            far = levels[np.abs(levels - a[p, g]) >= 10]
            a[p, g + 8] = far[np.random.randint(len(far))]
    return np.exp2(a.ravel()).repeat(32)


BF16 = ml_dtypes.bfloat16


def bf(x):
    return np.asarray(x, np.float32).astype(BF16)


def f64(x):
    return np.asarray(x).astype(np.float64)


N1, N2, D = 2048, 2048, 512

SQRT5 = np.sqrt(5.0)


def distance(X1, X2, l):
    A = f64(X1) / f64(l)
    B = f64(X2) / f64(l)
    sq1 = np.sum(A * A, axis=-1)
    sq2 = np.sum(B * B, axis=-1)
    d2 = np.maximum(sq1[:, None] + sq2[None, :] - 2.0 * (A @ B.T), 0.0)
    return np.sqrt(d2)


def setup_inputs():
    s = mx_kscale(N1)
    u = mx_kscale(N2)
    top = np.max(u)
    low = np.min(s)
    g = np.random.standard_normal((1, D))
    x1 = bf(np.random.standard_normal((N1, 1)) * g + 0.6 * np.random.standard_normal((N1, D)))
    x2 = bf(np.random.standard_normal((N2, 1)) * g + 0.6 * np.random.standard_normal((N2, D)))
    c = bf(np.random.uniform(size=(1,)) + 0.5)
    l = bf((np.random.uniform(size=(D,)) + 0.5) * 2.0 * np.sqrt(D))
    go = bf(np.random.standard_normal((N1, N2)) * np.exp2(np.random.randint(-6, 1, (N1, 1))) * 256.0 / s[:, None] * u[None, :])
    r = distance(x1, x2, l)
    return {"X1": bf(f64(x1) * s[:, None] / top), "X2": bf(f64(x2) / u[:, None] * low), "c": c, "l": l,
            "r": np.asarray(r, np.float32), "grad_out": go}


def reference(X1, X2, c, l, r, grad_out):
    rf = f64(r)
    c2 = np.squeeze(f64(c) * f64(c))
    G = f64(grad_out) * ((-5.0 / 6.0) * c2 * (1.0 + SQRT5 * rf) * np.exp(-SQRT5 * rf))
    rowsum = np.sum(G, axis=1)
    cs = np.sum(G, axis=0)
    Gb = G
    P = mxq(Gb, 1, "e5m2") @ mxq(f64(X2), 0, "e4m3")
    M = mxq(Gb, 0, "e5m2").T @ mxq(f64(X1), 0, "e4m3")
    lf = f64(l)
    k = (2.0 / (lf * lf))[None, :]
    dX1 = k * (f64(X1) * rowsum[:, None] - P)
    dX2 = k * (f64(X2) * cs[:, None] - M)
    return dX1, dX2

@@ -1,0 +1,297 @@
+from contextlib import ExitStack
+import math
+
+import concourse.mybir as mybir
+from concourse.masks import make_identity
+
+N1, N2, D = 2048, 2048, 512
+FLOPS = 2 * 2 * N1 * N2 * D
+
+F32 = mybir.dt.float32
+BF16 = mybir.dt.bfloat16
+U32 = mybir.dt.uint32
+U8 = mybir.dt.uint8
+E4 = mybir.dt.float8_e4m3fn_x4
+E5 = mybir.dt.float8_e5m2_x4
+ALU = mybir.AluOpType
+ACT = mybir.ActivationFunctionType
+AX = mybir.AxisListType
+
+P = 128
+SQRT5 = math.sqrt(5.0)
+NB = 16
+
+
+def tile_matern52_v_kernel(tc, X1, X2, c, l, r, grad_out, out_0, out_1):
+    nc = tc.nc
+    r_v = r.rearrange("(g p j) m -> p g j m", g=4, j=4)
+    go_v = grad_out.rearrange("(g p j) m -> p g j m", g=4, j=4)
+    x1_v = X1.rearrange("(g p j) d -> p g j d", g=4, j=4)
+    x2_v = X2.rearrange("(g p j) d -> p g j d", g=4, j=4)
+    o0_v = out_0.rearrange("(g p j) d -> p g j d", g=4, j=4)
+
+    with ExitStack() as ctx:
+        keep = ctx.enter_context(tc.tile_pool(name="keep", bufs=1))
+        work = ctx.enter_context(tc.tile_pool(name="work", bufs=2))
+        psum = ctx.enter_context(tc.psum_pool(name="psum", bufs=1))
+        ctx.enter_context(tc.manual_schedule())
+
+        warm = keep.tile([P, 1], F32, name="warm")
+        nc.vector.memset(warm[:], 0.0)
+        nc.scalar.activation(out=warm[:], in_=warm[:], func=ACT.Exp)
+        c_bf = keep.tile([P, 1], BF16, name="c_bf")
+        nc.gpsimd.dma_start(out=c_bf[:], in_=c.partition_broadcast(P))
+        l_bf = keep.tile([P, 4], BF16, name="l_bf")
+        with nc.allow_non_contiguous_dma(reason="512 lengthscales, one element a piece, once"):
+            nc.gpsimd.dma_start(out=l_bf[:], in_=l.rearrange("(f p) -> p f", p=P))
+        ident = keep.tile([P, P], F32, name="ident")
+        make_identity(nc, ident[:])
+        ones = keep.tile([P, 2], F32, name="ones")
+        nc.vector.memset(ones[:], 1.0)
+
+        x1raw = keep.tile([P, 4, 4, D], BF16, name="x1raw")
+        x1c = keep.tile([P, 4, D], U32, name="x1c", align_bytes=64)
+        x1s = keep.tile([P, 4, D], U8, name="x1s", align_bytes=64)
+        x2c = keep.tile([P, 4, D], U32, name="x2c", align_bytes=64)
+        x2s = keep.tile([P, 4, D], U8, name="x2s", align_bytes=64)
+        cM = keep.tile([P, 4, N2], U32, name="cM", align_bytes=64)
+        sM = keep.tile([P, 4, N2], U8, name="sM", align_bytes=64)
+        rs_part = keep.tile([P, 16, 4], F32, name="rs_part")
+        rs = keep.tile([P, 16], F32, name="rs")
+        cs = keep.tile([P, 16], F32, name="cs")
+        kc = keep.tile([P, 1], F32, name="kc")
+        k4 = keep.tile([P, 4], F32, name="k4")
+        ktile = keep.tile([P, D], F32, name="ktile")
+        cs_ps = psum.tile([P, 64, 2], F32, name="cs_ps", tag="cs_ps", bufs=1)
+
+        st = {}
+
+        def load(b):
+            g, mc = divmod(b, 4)
+            rt = work.tile([P, 4, 512], F32, name="rt", tag="rt", bufs=3)
+            nc.sync.dma_start(out=rt[:], in_=r_v[:, g, :, mc * 512:(mc + 1) * 512])
+            gt = work.tile([P, 4, 512], BF16, name="gt", tag="gt", bufs=3)
+            nc.sync.dma_start(out=gt[:], in_=go_v[:, g, :, mc * 512:(mc + 1) * 512])
+            st[("rt", b)] = rt
+            st[("gt", b)] = gt
+
+        def stage_a(b, h):
+            if h == 0:
+                st[("G", b)] = work.tile([P, 4, 512], F32, name="gblk", tag="gblk", bufs=4)
+            G = st[("G", b)]
+            rt = st[("rt", b)]
+            nc.scalar.activation(out=G[:, 2 * h:2 * h + 2, :], in_=rt[:, 2 * h:2 * h + 2, :],
+                                 func=ACT.Exp, scale=-SQRT5)
+
+        def stage_b(b):
+            G = st[("G", b)]
+            rt = st[("rt", b)]
+            nc.vector.scalar_tensor_tensor(out=G[:], in0=rt[:], scalar=1.0 / SQRT5, in1=G[:],
+                                           op0=ALU.add, op1=ALU.mult)
+
+        def stage_c(b):
+            g, mc = divmod(b, 4)
+            G = st[("G", b)]
+            gt = st[("gt", b)]
+            for j in range(4):
+                nc.vector.scalar_tensor_tensor(out=G[:, j, :], in0=G[:, j, :], scalar=kc[:, 0:1],
+                                               in1=gt[:, j, :], op0=ALU.mult, op1=ALU.mult,
+                                               accum_out=rs_part[:, 4 * g + j, mc:mc + 1])
+
+        def stage_t(b, j):
+            G = st[("G", b)]
+            pt = psum.tile([P, 4, P], F32, name="pt", tag="pt", bufs=3)
+            for t in range(4):
+                nc.tensor.transpose(pt[:, t, :], G[:, j, t:512:4], ident[:])
+            st[("pt", b, j)] = pt
+
+        def stage_e(b, j):
+            if j == 0:
+                st[("fm", b)] = work.tile([P, 4, P, 4], BF16, name="fm", tag="fm", bufs=2, align_bytes=64)
+            fm = st[("fm", b)]
+            pt = st[("pt", b, j)]
+            nc.scalar.copy(out=fm[:, j, :, :], in_=pt[:].rearrange("p t n -> p n t"))
+
+        def stage_cs(b, q):
+            G = st[("G", b)]
+            for j in range(4):
+                nc.tensor.matmul(out=cs_ps[:, 4 * b + q, :], lhsT=G[:, j, q * P:(q + 1) * P], rhs=ones[:],
+                                 start=(j == 0), stop=(j == 3))
+
+        def stage_d(b, h):
+            if h == 0:
+                st[("tm", b)] = work.tile([P, 512, 4], BF16, name="tm", tag="tm", bufs=2, align_bytes=64)
+            tm = st[("tm", b)]
+            G = st[("G", b)]
+            nc.scalar.copy(out=tm[:, 256 * h:256 * h + 256, :],
+                           in_=G[:, :, 256 * h:256 * h + 256].rearrange("p t c -> p c t"))
+
+        def stage_q(b):
+            g, mc = divmod(b, 4)
+            if mc == 0:
+                st[("cP", g)] = work.tile([P, 4, 512], U32, name="cP", tag="cP", bufs=2, align_bytes=64)
+                st[("sP", g)] = work.tile([P, 4, 512], U8, name="sP", tag="sP", bufs=2, align_bytes=64)
+            cP = st[("cP", g)]
+            sP = st[("sP", g)]
+            nc.vector.quantize_mx(out=cP[:, mc, :].bitcast(E5), scales=sP[:, mc, :],
+                                  in_=st[("fm", b)][:].rearrange("p j n t -> p (j n t)"))
+            nc.vector.quantize_mx(out=cM[:, g, mc * 512:(mc + 1) * 512].bitcast(E5),
+                                  scales=sM[:, g, mc * 512:(mc + 1) * 512],
+                                  in_=st[("tm", b)][:].rearrange("p c t -> p (c t)"))
+
+        def burst_p(g):
+            cP = st[("cP", g)]
+            sP = st[("sP", g)]
+            for j in range(4):
+                acc = psum.tile([P, D], F32, name="acc", tag="acc", bufs=4)
+                for mc in range(4):
+                    nc.tensor.matmul_mx(out=acc[:], lhsT=cP[:, mc, j * P:(j + 1) * P].bitcast(E5),
+                                        lhsT_scale=sP[:, mc, j * P:(j + 1) * P],
+                                        rhs=x2c[:, mc, :].bitcast(E4), rhs_scale=x2s[:, mc, :],
+                                        start=(mc == 0), stop=(mc == 3))
+                st[("accP", g, j)] = acc
+
+        def burst_m(mc):
+            for q in range(4):
+                lo = mc * 512 + q * P
+                acc = psum.tile([P, D], F32, name="acc", tag="acc", bufs=4)
+                for g in range(4):
+                    nc.tensor.matmul_mx(out=acc[:], lhsT=cM[:, g, lo:lo + P].bitcast(E5),
+                                        lhsT_scale=sM[:, g, lo:lo + P],
+                                        rhs=x1c[:, g, :].bitcast(E4), rhs_scale=x1s[:, g, :],
+                                        start=(g == 0), stop=(g == 3))
+                st[("accM", mc, q)] = acc
+
+        def epilogue(items):
+            zs = []
+            n = len(items)
+            for i in range(n + 1):
+                if i < n:
+                    x_ap, s_ap, acc, key = items[i]
+                    z = work.tile([P, D], F32, name="z", tag="z", bufs=3)
+                    nc.vector.scalar_tensor_tensor(out=z[:], in0=x_ap, scalar=s_ap, in1=acc[:],
+                                                   op0=ALU.mult, op1=ALU.subtract)
+                    zs.append(z)
+                if i > 0:
+                    key = items[i - 1][3]
+                    o = work.tile([P, D], F32, name="o", tag="o", bufs=4)
+                    nc.vector.tensor_tensor(out=o[:], in0=zs[i - 1][:], in1=ktile[:], op=ALU.mult)
+                    st[("o", key)] = o
+
+        def h_p(g):
+            nc.vector.tensor_reduce(out=rs[:, 4 * g:4 * g + 4], in_=rs_part[:, 4 * g:4 * g + 4, :],
+                                    axis=AX.X, op=ALU.add)
+            epilogue([(x1raw[:, g, j, :], rs[:, 4 * g + j:4 * g + j + 1], st[("accP", g, j)], ("p", g, j))
+                      for j in range(4)])
+
+        def store_p(g):
+            for j in range(4):
+                nc.sync.dma_start(out=o0_v[:, g, j, :], in_=st[("o", ("p", g, j))][:])
+
+        def load_x2n(mc):
+            for q in range(4):
+                x2n = work.tile([P, D], BF16, name="x2n", tag="x2n", bufs=4)
+                lo = mc * 512 + q * P
+                nc.gpsimd.dma_start(out=x2n[:], in_=X2[lo:lo + P, :])
+                st[("x2n", mc, q)] = x2n
+
+        def h_m(mc):
+            view = cs_ps[:].rearrange("p (g a q) two -> p a q g two", g=4, a=4)
+            nc.vector.tensor_reduce(out=cs[:, 4 * mc:4 * mc + 4], in_=view[:, mc, :, :, 0],
+                                    axis=AX.X, op=ALU.add)
+            epilogue([(st[("x2n", mc, q)][:], cs[:, 4 * mc + q:4 * mc + q + 1], st[("accM", mc, q)], ("m", mc, q))
+                      for q in range(4)])
+
+        def store_m(mc):
+            for q in range(4):
+                lo = mc * 512 + q * P
+                nc.sync.dma_start(out=out_1[lo:lo + P, :], in_=st[("o", ("m", mc, q))][:])
+
+        def x_group(src, eng):
+            xg = work.tile([P, D, 4], BF16, name="xg", tag="xg", bufs=2, align_bytes=64)
+            if eng == 0:
+                nc.vector.tensor_copy(out=xg[:], in_=src.rearrange("p j d -> p d j"))
+            else:
+                nc.scalar.copy(out=xg[:], in_=src.rearrange("p j d -> p d j"))
+            return xg
+
+        def x_quant(xg, codes, scales):
+            nc.vector.quantize_mx(out=codes.bitcast(E4), scales=scales,
+                                  in_=xg[:].rearrange("p d j -> p (d j)"))
+
+        for i in range(-1, NB + 3):
+            if i == -1:
+                load(0)
+                load(1)
+            if i + 2 < NB:
+                load(i + 2)
+            if 0 <= i < 4:
+                x2r = work.tile([P, 4, D], BF16, name="x2r", tag="x2r", bufs=2)
+                nc.sync.dma_start(out=x2r[:], in_=x2_v[:, i, :, :])
+                st[("x2r", i)] = x2r
+                nc.sync.dma_start(out=x1raw[:, i, :, :], in_=x1_v[:, i, :, :])
+            if 13 <= i < 17:
+                load_x2n(i - 13)
+            if i == 0:
+                nc.vector.tensor_tensor(out=kc[:], in0=c_bf[:], in1=c_bf[:], op=ALU.mult)
+                nc.vector.tensor_scalar_mul(out=kc[:], in0=kc[:], scalar1=-5.0 / 6.0 * SQRT5)
+                nc.vector.tensor_tensor(out=k4[:], in0=l_bf[:], in1=l_bf[:], op=ALU.mult)
+                nc.vector.reciprocal(out=k4[:], in_=k4[:])
+                nc.vector.tensor_scalar_mul(out=k4[:], in0=k4[:], scalar1=2.0)
+                kp = psum.tile([P, D], F32, name="acc", tag="acc", bufs=4)
+                for f in range(4):
+                    nc.tensor.matmul(out=kp[:, f * P:(f + 1) * P], lhsT=k4[:, f:f + 1].to_broadcast([P, P]),
+                                     rhs=ident[:], start=True, stop=True)
+            if i + 1 < NB:
+                stage_a(i + 1, 0)
+            tb = i - 1
+            has_t = 0 <= tb < NB
+            if has_t:
+                stage_t(tb, 0)
+                stage_t(tb, 1)
+                stage_cs(tb, 0)
+                stage_cs(tb, 1)
+            if 0 <= i - 2 < NB:
+                stage_q(i - 2)
+            if 0 <= i < NB:
+                stage_b(i)
+            if has_t:
+                stage_e(tb, 0)
+                stage_e(tb, 1)
+                stage_t(tb, 2)
+                stage_t(tb, 3)
+                stage_cs(tb, 2)
+                stage_cs(tb, 3)
+                stage_d(tb, 0)
+            if 0 <= i < NB:
+                stage_c(i)
+            if has_t:
+                stage_e(tb, 2)
+                stage_e(tb, 3)
+                stage_d(tb, 1)
+            if i + 1 < NB:
+                stage_a(i + 1, 1)
+            if i == 0:
+                nc.vector.tensor_copy(out=ktile[:], in_=kp[:])
+            if 1 <= i < 5:
+                st[("x2g", i - 1)] = x_group(st[("x2r", i - 1)][:], 0)
+            if 2 <= i < 6:
+                x_quant(st[("x2g", i - 2)], x2c[:, i - 2, :], x2s[:, i - 2, :])
+            if 10 <= i < 14:
+                st[("x1g", i - 10)] = x_group(x1raw[:, i - 10, :, :], 1)
+            if 11 <= i < 15:
+                x_quant(st[("x1g", i - 11)], x1c[:, i - 11, :], x1s[:, i - 11, :])
+            pb = i - 3
+            if 0 <= pb < NB and pb % 4 == 3:
+                h_p(pb // 4)
+            if 12 <= pb < NB:
+                h_m(pb - 12)
+            if 0 <= pb < NB and pb % 4 == 3:
+                store_p(pb // 4)
+            if 12 <= pb < NB:
+                store_m(pb - 12)
+            qb = i - 2
+            if 0 <= qb < NB and qb % 4 == 3:
+                burst_p(qb // 4)
+            if 12 <= qb < NB:
+                burst_m(qb - 12)

@@ -40,14 +40,13 @@ def tile_matern52_v_kernel(tc, X1, X2, c, l, r, grad_out, out_0, out_1):
         nc.vector.memset(warm[:], 0.0)
         nc.scalar.activation(out=warm[:], in_=warm[:], func=ACT.Exp)
         c_bf = keep.tile([P, 1], BF16, name="c_bf")
-        nc.gpsimd.dma_start(out=c_bf[:], in_=c.partition_broadcast(P))
+        nc.scalar.dma_start(out=c_bf[:], in_=c.partition_broadcast(P))
         l_bf = keep.tile([P, 4], BF16, name="l_bf")
         with nc.allow_non_contiguous_dma(reason="512 lengthscales, one element a piece, once"):
             nc.gpsimd.dma_start(out=l_bf[:], in_=l.rearrange("(f p) -> p f", p=P))
         ident = keep.tile([P, P], F32, name="ident")
         make_identity(nc, ident[:])
-        ones = keep.tile([P, 2], F32, name="ones")
-        nc.vector.memset(ones[:], 1.0)
+        junk = keep.tile([P, P], BF16, name="junk")
 
         x1raw = keep.tile([P, 4, 4, D], BF16, name="x1raw")
         x1c = keep.tile([P, 4, D], U32, name="x1c", align_bytes=64)
@@ -62,14 +61,18 @@ def tile_matern52_v_kernel(tc, X1, X2, c, l, r, grad_out, out_0, out_1):
         kc = keep.tile([P, 1], F32, name="kc")
         k4 = keep.tile([P, 4], F32, name="k4")
         ktile = keep.tile([P, D], F32, name="ktile")
-        cs_ps = psum.tile([P, 64, 2], F32, name="cs_ps", tag="cs_ps", bufs=1)
+        cs_part = keep.tile([P, 4, 16], F32, name="cs_part")
 
         st = {}
 
         def load(b):
             g, mc = divmod(b, 4)
             rt = work.tile([P, 4, 512], F32, name="rt", tag="rt", bufs=3)
-            nc.sync.dma_start(out=rt[:], in_=r_v[:, g, :, mc * 512:(mc + 1) * 512])
+            if b == 0:
+                for h in range(2):
+                    nc.sync.dma_start(out=rt[:, 2 * h:2 * h + 2, :], in_=r_v[:, g, 2 * h:2 * h + 2, 0:512])
+            else:
+                nc.sync.dma_start(out=rt[:], in_=r_v[:, g, :, mc * 512:(mc + 1) * 512])
             gt = work.tile([P, 4, 512], BF16, name="gt", tag="gt", bufs=3)
             nc.sync.dma_start(out=gt[:], in_=go_v[:, g, :, mc * 512:(mc + 1) * 512])
             st[("rt", b)] = rt
@@ -98,25 +101,39 @@ def tile_matern52_v_kernel(tc, X1, X2, c, l, r, grad_out, out_0, out_1):
                                                in1=gt[:, j, :], op0=ALU.mult, op1=ALU.mult,
                                                accum_out=rs_part[:, 4 * g + j, mc:mc + 1])
 
-        def stage_t(b, j):
-            G = st[("G", b)]
-            pt = psum.tile([P, 4, P], F32, name="pt", tag="pt", bufs=3)
+        def stage_t(b, u):
+            tmw = st[("tm", b)][:].rearrange("p c t -> p (c t)").bitcast(F32)
+            pt = psum.tile([P, 4, P], F32, name="pt", tag="pt", bufs=2)
             for t in range(4):
-                nc.tensor.transpose(pt[:, t, :], G[:, j, t:512:4], ident[:])
-            st[("pt", b, j)] = pt
+                nc.tensor.transpose(pt[:, t, :], tmw[:, 2 * t + u:1024:8], ident[:])
+            st[("pt", b, u)] = pt
 
-        def stage_e(b, j):
-            if j == 0:
+        def stage_e(b, u):
+            if u == 0:
                 st[("fm", b)] = work.tile([P, 4, P, 4], BF16, name="fm", tag="fm", bufs=2, align_bytes=64)
             fm = st[("fm", b)]
-            pt = st[("pt", b, j)]
-            nc.scalar.copy(out=fm[:, j, :, :], in_=pt[:].rearrange("p t n -> p n t"))
+            pt = st[("pt", b, u)]
+            src = pt[:].rearrange("q t p -> q (t p)").bitcast(BF16)
+            nc.scalar.copy(out=fm[:, 2 * u:2 * u + 2, :, :],
+                           in_=src.rearrange("q (t p e) -> q e p t", t=4, e=2))
 
         def stage_cs(b, q):
             G = st[("G", b)]
+            if q == 0:
+                st[("csp", b)] = psum.tile([P, 4, P], F32, name="csp", tag="csp", bufs=2)
+            csp = st[("csp", b)]
             for j in range(4):
-                nc.tensor.matmul(out=cs_ps[:, 4 * b + q, :], lhsT=G[:, j, q * P:(q + 1) * P], rhs=ones[:],
-                                 start=(j == 0), stop=(j == 3))
+                nc.tensor.matmul(out=csp[:, q, :], lhsT=G[:, j, q * P:(q + 1) * P], rhs=ident[:],
+                                 is_transpose=True, start=(j == 0), stop=(j == 3))
+
+        def stage_cs_out(b):
+            g, mc = divmod(b, 4)
+            csp = st[("csp", b)]
+            if b < 12:
+                nc.vector.tensor_reduce(out=cs_part[:, g, 4 * mc:4 * mc + 4], in_=csp[:], axis=AX.X, op=ALU.add)
+            for q in range(4 if b >= 12 else 0):
+                nc.scalar.activation(out=junk[:], in_=csp[:, q, :], func=ACT.Copy,
+                                     accum_out=cs_part[:, g, 4 * mc + q:4 * mc + q + 1])
 
         def stage_d(b, h):
             if h == 0:
@@ -196,8 +213,8 @@ def tile_matern52_v_kernel(tc, X1, X2, c, l, r, grad_out, out_0, out_1):
                 st[("x2n", mc, q)] = x2n
 
         def h_m(mc):
-            view = cs_ps[:].rearrange("p (g a q) two -> p a q g two", g=4, a=4)
-            nc.vector.tensor_reduce(out=cs[:, 4 * mc:4 * mc + 4], in_=view[:, mc, :, :, 0],
+            nc.vector.tensor_reduce(out=cs[:, 4 * mc:4 * mc + 4],
+                                    in_=cs_part[:, :, 4 * mc:4 * mc + 4].rearrange("p g q -> p q g"),
                                     axis=AX.X, op=ALU.add)
             epilogue([(st[("x2n", mc, q)][:], cs[:, 4 * mc + q:4 * mc + q + 1], st[("accM", mc, q)], ("m", mc, q))
                       for q in range(4)])
@@ -222,7 +239,6 @@ def tile_matern52_v_kernel(tc, X1, X2, c, l, r, grad_out, out_0, out_1):
         for i in range(-1, NB + 3):
             if i == -1:
                 load(0)
-                load(1)
             if i + 2 < NB:
                 load(i + 2)
             if 0 <= i < 4:
@@ -235,6 +251,7 @@ def tile_matern52_v_kernel(tc, X1, X2, c, l, r, grad_out, out_0, out_1):
             if i == 0:
                 nc.vector.tensor_tensor(out=kc[:], in0=c_bf[:], in1=c_bf[:], op=ALU.mult)
                 nc.vector.tensor_scalar_mul(out=kc[:], in0=kc[:], scalar1=-5.0 / 6.0 * SQRT5)
+            if i == 3:
                 nc.vector.tensor_tensor(out=k4[:], in0=l_bf[:], in1=l_bf[:], op=ALU.mult)
                 nc.vector.reciprocal(out=k4[:], in_=k4[:])
                 nc.vector.tensor_scalar_mul(out=k4[:], in0=k4[:], scalar1=2.0)
@@ -242,36 +259,30 @@ def tile_matern52_v_kernel(tc, X1, X2, c, l, r, grad_out, out_0, out_1):
                 for f in range(4):
                     nc.tensor.matmul(out=kp[:, f * P:(f + 1) * P], lhsT=k4[:, f:f + 1].to_broadcast([P, P]),
                                      rhs=ident[:], start=True, stop=True)
-            if i + 1 < NB:
-                stage_a(i + 1, 0)
             tb = i - 1
             has_t = 0 <= tb < NB
             if has_t:
-                stage_t(tb, 0)
-                stage_t(tb, 1)
-                stage_cs(tb, 0)
-                stage_cs(tb, 1)
+                stage_d(tb, 0)
+                stage_d(tb, 1)
+                for q in range(4):
+                    stage_cs(tb, q)
             if 0 <= i - 2 < NB:
                 stage_q(i - 2)
             if 0 <= i < NB:
                 stage_b(i)
+            if i + 1 < NB:
+                stage_a(i + 1, 0)
+                stage_a(i + 1, 1)
             if has_t:
-                stage_e(tb, 0)
-                stage_e(tb, 1)
-                stage_t(tb, 2)
-                stage_t(tb, 3)
-                stage_cs(tb, 2)
-                stage_cs(tb, 3)
-                stage_d(tb, 0)
+                stage_t(tb, 0)
+                stage_t(tb, 1)
+                stage_cs_out(tb)
             if 0 <= i < NB:
                 stage_c(i)
             if has_t:
-                stage_e(tb, 2)
-                stage_e(tb, 3)
-                stage_d(tb, 1)
-            if i + 1 < NB:
-                stage_a(i + 1, 1)
-            if i == 0:
+                stage_e(tb, 0)
+                stage_e(tb, 1)
+            if i == 3:
                 nc.vector.tensor_copy(out=ktile[:], in_=kp[:])
             if 1 <= i < 5:
                 st[("x2g", i - 1)] = x_group(st[("x2r", i - 1)][:], 0)

@@ -20,14 +20,18 @@ AX = mybir.AxisListType
 P = 128
 SQRT5 = math.sqrt(5.0)
 NB = 16
+R_ON_VECTOR = 0
+X1_ON_VECTOR = 2
 
 
 def tile_matern52_v_kernel(tc, X1, X2, c, l, r, grad_out, out_0, out_1):
     nc = tc.nc
+    ORDER = [(g, mc) for g in range(2) for mc in range(4)] + [(g, mc) for mc in range(4) for g in (2, 3)]
     r_v = r.rearrange("(g p j) m -> p g j m", g=4, j=4)
     go_v = grad_out.rearrange("(g p j) m -> p g j m", g=4, j=4)
     x1_v = X1.rearrange("(g p j) d -> p g j d", g=4, j=4)
     x2_v = X2.rearrange("(g p j) d -> p g j d", g=4, j=4)
+    x2n_v = X2.rearrange("(a p) d -> p a d", p=P)
     o0_v = out_0.rearrange("(g p j) d -> p g j d", g=4, j=4)
 
     with ExitStack() as ctx:
@@ -36,11 +40,11 @@ def tile_matern52_v_kernel(tc, X1, X2, c, l, r, grad_out, out_0, out_1):
         psum = ctx.enter_context(tc.psum_pool(name="psum", bufs=1))
         ctx.enter_context(tc.manual_schedule())
 
+        c_bf = keep.tile([P, 1], BF16, name="c_bf")
+        nc.scalar.dma_start(out=c_bf[:], in_=c.partition_broadcast(P))
         warm = keep.tile([P, 1], F32, name="warm")
         nc.vector.memset(warm[:], 0.0)
         nc.scalar.activation(out=warm[:], in_=warm[:], func=ACT.Exp)
-        c_bf = keep.tile([P, 1], BF16, name="c_bf")
-        nc.scalar.dma_start(out=c_bf[:], in_=c.partition_broadcast(P))
         l_bf = keep.tile([P, 4], BF16, name="l_bf")
         with nc.allow_non_contiguous_dma(reason="512 lengthscales, one element a piece, once"):
             nc.gpsimd.dma_start(out=l_bf[:], in_=l.rearrange("(f p) -> p f", p=P))
@@ -49,6 +53,7 @@ def tile_matern52_v_kernel(tc, X1, X2, c, l, r, grad_out, out_0, out_1):
         junk = keep.tile([P, P], BF16, name="junk")
 
         x1raw = keep.tile([P, 4, 4, D], BF16, name="x1raw")
+        x2n = keep.tile([P, 16, D], BF16, name="x2n")
         x1c = keep.tile([P, 4, D], U32, name="x1c", align_bytes=64)
         x1s = keep.tile([P, 4, D], U8, name="x1s", align_bytes=64)
         x2c = keep.tile([P, 4, D], U32, name="x2c", align_bytes=64)
@@ -57,43 +62,46 @@ def tile_matern52_v_kernel(tc, X1, X2, c, l, r, grad_out, out_0, out_1):
         sM = keep.tile([P, 4, N2], U8, name="sM", align_bytes=64)
         rs_part = keep.tile([P, 16, 4], F32, name="rs_part")
         rs = keep.tile([P, 16], F32, name="rs")
+        cs_part = keep.tile([P, 4, 16], F32, name="cs_part")
         cs = keep.tile([P, 16], F32, name="cs")
         kc = keep.tile([P, 1], F32, name="kc")
         k4 = keep.tile([P, 4], F32, name="k4")
         ktile = keep.tile([P, D], F32, name="ktile")
-        cs_part = keep.tile([P, 4, 16], F32, name="cs_part")
 
         st = {}
 
         def load(b):
-            g, mc = divmod(b, 4)
+            g, mc = ORDER[b]
+            cols = (mc * 512, (mc + 1) * 512)
             rt = work.tile([P, 4, 512], F32, name="rt", tag="rt", bufs=3)
             if b == 0:
                 for h in range(2):
                     nc.sync.dma_start(out=rt[:, 2 * h:2 * h + 2, :], in_=r_v[:, g, 2 * h:2 * h + 2, 0:512])
             else:
-                nc.sync.dma_start(out=rt[:], in_=r_v[:, g, :, mc * 512:(mc + 1) * 512])
+                nc.sync.dma_start(out=rt[:], in_=r_v[:, g, :, cols[0]:cols[1]])
             gt = work.tile([P, 4, 512], BF16, name="gt", tag="gt", bufs=3)
-            nc.sync.dma_start(out=gt[:], in_=go_v[:, g, :, mc * 512:(mc + 1) * 512])
+            nc.sync.dma_start(out=gt[:], in_=go_v[:, g, :, cols[0]:cols[1]])
             st[("rt", b)] = rt
             st[("gt", b)] = gt
 
-        def stage_a(b, h):
-            if h == 0:
-                st[("G", b)] = work.tile([P, 4, 512], F32, name="gblk", tag="gblk", bufs=4)
-            G = st[("G", b)]
+        def stage_a(b):
+            G = work.tile([P, 4, 512], F32, name="gblk", tag="gblk", bufs=3)
+            st[("G", b)] = G
             rt = st[("rt", b)]
-            nc.scalar.activation(out=G[:, 2 * h:2 * h + 2, :], in_=rt[:, 2 * h:2 * h + 2, :],
-                                 func=ACT.Exp, scale=-SQRT5)
+            if b == 0:
+                for h in range(2):
+                    nc.scalar.activation(out=G[:, 2 * h:2 * h + 2, :], in_=rt[:, 2 * h:2 * h + 2, :],
+                                         func=ACT.Exp, scale=-SQRT5)
+            else:
+                nc.scalar.activation(out=G[:], in_=rt[:], func=ACT.Exp, scale=-SQRT5)
 
         def stage_b(b):
             G = st[("G", b)]
-            rt = st[("rt", b)]
-            nc.vector.scalar_tensor_tensor(out=G[:], in0=rt[:], scalar=1.0 / SQRT5, in1=G[:],
+            nc.vector.scalar_tensor_tensor(out=G[:], in0=st[("rt", b)][:], scalar=1.0 / SQRT5, in1=G[:],
                                            op0=ALU.add, op1=ALU.mult)
 
         def stage_c(b):
-            g, mc = divmod(b, 4)
+            g, mc = ORDER[b]
             G = st[("G", b)]
             gt = st[("gt", b)]
             for j in range(4):
@@ -101,60 +109,59 @@ def tile_matern52_v_kernel(tc, X1, X2, c, l, r, grad_out, out_0, out_1):
                                                in1=gt[:, j, :], op0=ALU.mult, op1=ALU.mult,
                                                accum_out=rs_part[:, 4 * g + j, mc:mc + 1])
 
-        def stage_t(b, u):
-            tmw = st[("tm", b)][:].rearrange("p c t -> p (c t)").bitcast(F32)
-            pt = psum.tile([P, 4, P], F32, name="pt", tag="pt", bufs=2)
-            for t in range(4):
-                nc.tensor.transpose(pt[:, t, :], tmw[:, 2 * t + u:1024:8], ident[:])
-            st[("pt", b, u)] = pt
+        def stage_d(b):
+            tm = work.tile([P, 512, 4], BF16, name="tm", tag="tm", bufs=3, align_bytes=64)
+            st[("tm", b)] = tm
+            nc.scalar.copy(out=tm[:].rearrange("p (a i) t -> p a t i", i=4),
+                           in_=st[("G", b)][:].rearrange("p t (a i) -> p a t i", i=4))
 
-        def stage_e(b, u):
-            if u == 0:
-                st[("fm", b)] = work.tile([P, 4, P, 4], BF16, name="fm", tag="fm", bufs=2, align_bytes=64)
-            fm = st[("fm", b)]
-            pt = st[("pt", b, u)]
-            src = pt[:].rearrange("q t p -> q (t p)").bitcast(BF16)
-            nc.scalar.copy(out=fm[:, 2 * u:2 * u + 2, :, :],
-                           in_=src.rearrange("q (t p e) -> q e p t", t=4, e=2))
-
-        def stage_cs(b, q):
+        def stage_cs(b):
             G = st[("G", b)]
-            if q == 0:
-                st[("csp", b)] = psum.tile([P, 4, P], F32, name="csp", tag="csp", bufs=2)
-            csp = st[("csp", b)]
-            for j in range(4):
-                nc.tensor.matmul(out=csp[:, q, :], lhsT=G[:, j, q * P:(q + 1) * P], rhs=ident[:],
-                                 is_transpose=True, start=(j == 0), stop=(j == 3))
+            csp = psum.tile([P, 4, P], F32, name="csp", tag="csp", bufs=1)
+            st[("csp", b)] = csp
+            for q in range(4):
+                for j in range(4):
+                    nc.tensor.matmul(out=csp[:, q, :], lhsT=G[:, j, q * P:(q + 1) * P], rhs=ident[:],
+                                     is_transpose=True, start=(j == 0), stop=(j == 3))
 
-        def stage_cs_out(b):
-            g, mc = divmod(b, 4)
+        def stage_r(b):
+            g, mc = ORDER[b]
             csp = st[("csp", b)]
-            if b < 12:
+            if b < R_ON_VECTOR:
                 nc.vector.tensor_reduce(out=cs_part[:, g, 4 * mc:4 * mc + 4], in_=csp[:], axis=AX.X, op=ALU.add)
-            for q in range(4 if b >= 12 else 0):
+            for q in range(4 if b >= R_ON_VECTOR else 0):
                 nc.scalar.activation(out=junk[:], in_=csp[:, q, :], func=ACT.Copy,
                                      accum_out=cs_part[:, g, 4 * mc + q:4 * mc + q + 1])
 
-        def stage_d(b, h):
-            if h == 0:
-                st[("tm", b)] = work.tile([P, 512, 4], BF16, name="tm", tag="tm", bufs=2, align_bytes=64)
-            tm = st[("tm", b)]
-            G = st[("G", b)]
-            nc.scalar.copy(out=tm[:, 256 * h:256 * h + 256, :],
-                           in_=G[:, :, 256 * h:256 * h + 256].rearrange("p t c -> p c t"))
+        def stage_t(b):
+            tmw = st[("tm", b)][:].rearrange("p c t -> p (c t)").bitcast(F32)
+            for u in range(2):
+                pt = psum.tile([P, 4, P], F32, name="pt", tag="pt", bufs=3)
+                for t in range(4):
+                    nc.tensor.transpose(pt[:, t, :], tmw[:, 2 * t + u:1024:8], ident[:])
+                st[("pt", b, u)] = pt
 
-        def stage_q(b):
-            g, mc = divmod(b, 4)
-            if mc == 0:
-                st[("cP", g)] = work.tile([P, 4, 512], U32, name="cP", tag="cP", bufs=2, align_bytes=64)
-                st[("sP", g)] = work.tile([P, 4, 512], U8, name="sP", tag="sP", bufs=2, align_bytes=64)
-            cP = st[("cP", g)]
-            sP = st[("sP", g)]
-            nc.vector.quantize_mx(out=cP[:, mc, :].bitcast(E5), scales=sP[:, mc, :],
-                                  in_=st[("fm", b)][:].rearrange("p j n t -> p (j n t)"))
+        def stage_e(b):
+            fm = work.tile([P, 4, P, 4], BF16, name="fm", tag="fm", bufs=2, align_bytes=64)
+            st[("fm", b)] = fm
+            for u in range(2):
+                src = st[("pt", b, u)][:].rearrange("q t p -> q (t p)").bitcast(BF16)
+                nc.scalar.copy(out=fm[:, 2 * u:2 * u + 2, :, :],
+                               in_=src.rearrange("q (t p e) -> q e p t", t=4, e=2))
+
+        def stage_qm(b):
+            g, mc = ORDER[b]
             nc.vector.quantize_mx(out=cM[:, g, mc * 512:(mc + 1) * 512].bitcast(E5),
                                   scales=sM[:, g, mc * 512:(mc + 1) * 512],
                                   in_=st[("tm", b)][:].rearrange("p c t -> p (c t)"))
+
+        def stage_qp(b):
+            g, mc = ORDER[b]
+            if mc == 0:
+                st[("cP", g)] = work.tile([P, 4, 512], U32, name="cP", tag="cP", bufs=2, align_bytes=64)
+                st[("sP", g)] = work.tile([P, 4, 512], U8, name="sP", tag="sP", bufs=2, align_bytes=64)
+            nc.vector.quantize_mx(out=st[("cP", g)][:, mc, :].bitcast(E5), scales=st[("sP", g)][:, mc, :],
+                                  in_=st[("fm", b)][:].rearrange("p j n t -> p (j n t)"))
 
         def burst_p(g):
             cP = st[("cP", g)]
@@ -181,62 +188,48 @@ def tile_matern52_v_kernel(tc, X1, X2, c, l, r, grad_out, out_0, out_1):
 
         def epilogue(items):
             zs = []
-            n = len(items)
-            for i in range(n + 1):
-                if i < n:
-                    x_ap, s_ap, acc, key = items[i]
-                    z = work.tile([P, D], F32, name="z", tag="z", bufs=3)
-                    nc.vector.scalar_tensor_tensor(out=z[:], in0=x_ap, scalar=s_ap, in1=acc[:],
-                                                   op0=ALU.mult, op1=ALU.subtract)
-                    zs.append(z)
-                if i > 0:
-                    key = items[i - 1][3]
-                    o = work.tile([P, D], F32, name="o", tag="o", bufs=4)
-                    nc.vector.tensor_tensor(out=o[:], in0=zs[i - 1][:], in1=ktile[:], op=ALU.mult)
-                    st[("o", key)] = o
+            for x_ap, s_ap, acc, dst in items:
+                z = work.tile([P, D], F32, name="z", tag="z", bufs=4)
+                nc.vector.scalar_tensor_tensor(out=z[:], in0=x_ap, scalar=s_ap, in1=acc[:],
+                                               op0=ALU.mult, op1=ALU.subtract)
+                zs.append(z)
+            for i in (0, 2, 1, 3):
+                o = work.tile([P, D], F32, name="o", tag="o", bufs=4)
+                if i < 2:
+                    nc.gpsimd.tensor_tensor(out=o[:], in0=zs[i][:], in1=ktile[:], op=ALU.mult)
+                else:
+                    nc.vector.tensor_tensor(out=o[:], in0=zs[i][:], in1=ktile[:], op=ALU.mult)
+                nc.sync.dma_start(out=items[i][3], in_=o[:])
 
         def h_p(g):
             nc.vector.tensor_reduce(out=rs[:, 4 * g:4 * g + 4], in_=rs_part[:, 4 * g:4 * g + 4, :],
                                     axis=AX.X, op=ALU.add)
-            epilogue([(x1raw[:, g, j, :], rs[:, 4 * g + j:4 * g + j + 1], st[("accP", g, j)], ("p", g, j))
+            epilogue([(x1raw[:, g, j, :], rs[:, 4 * g + j:4 * g + j + 1], st[("accP", g, j)], o0_v[:, g, j, :])
                       for j in range(4)])
-
-        def store_p(g):
-            for j in range(4):
-                nc.sync.dma_start(out=o0_v[:, g, j, :], in_=st[("o", ("p", g, j))][:])
-
-        def load_x2n(mc):
-            for q in range(4):
-                x2n = work.tile([P, D], BF16, name="x2n", tag="x2n", bufs=4)
-                lo = mc * 512 + q * P
-                nc.gpsimd.dma_start(out=x2n[:], in_=X2[lo:lo + P, :])
-                st[("x2n", mc, q)] = x2n
 
         def h_m(mc):
             nc.vector.tensor_reduce(out=cs[:, 4 * mc:4 * mc + 4],
                                     in_=cs_part[:, :, 4 * mc:4 * mc + 4].rearrange("p g q -> p q g"),
                                     axis=AX.X, op=ALU.add)
-            epilogue([(st[("x2n", mc, q)][:], cs[:, 4 * mc + q:4 * mc + q + 1], st[("accM", mc, q)], ("m", mc, q))
-                      for q in range(4)])
+            epilogue([(x2n[:, 4 * mc + q, :], cs[:, 4 * mc + q:4 * mc + q + 1], st[("accM", mc, q)],
+                       out_1[(4 * mc + q) * P:(4 * mc + q + 1) * P, :]) for q in range(4)])
 
-        def store_m(mc):
-            for q in range(4):
-                lo = mc * 512 + q * P
-                nc.sync.dma_start(out=out_1[lo:lo + P, :], in_=st[("o", ("m", mc, q))][:])
-
-        def x_group(src, eng):
+        def x_group(src, on_vector):
             xg = work.tile([P, D, 4], BF16, name="xg", tag="xg", bufs=2, align_bytes=64)
-            if eng == 0:
-                nc.vector.tensor_copy(out=xg[:], in_=src.rearrange("p j d -> p d j"))
+            dst_v = xg[:].rearrange("p (a i) j -> p a j i", i=4)
+            src_v = src.rearrange("p j (a i) -> p a j i", i=4)
+            if on_vector:
+                nc.vector.tensor_copy(out=dst_v, in_=src_v)
             else:
-                nc.scalar.copy(out=xg[:], in_=src.rearrange("p j d -> p d j"))
+                nc.scalar.copy(out=dst_v, in_=src_v)
             return xg
 
         def x_quant(xg, codes, scales):
             nc.vector.quantize_mx(out=codes.bitcast(E4), scales=scales,
                                   in_=xg[:].rearrange("p d j -> p (d j)"))
 
-        for i in range(-1, NB + 3):
+        pend_h = []
+        for i in range(-1, NB + 4):
             if i == -1:
                 load(0)
             if i + 2 < NB:
@@ -246,11 +239,34 @@ def tile_matern52_v_kernel(tc, X1, X2, c, l, r, grad_out, out_0, out_1):
                 nc.sync.dma_start(out=x2r[:], in_=x2_v[:, i, :, :])
                 st[("x2r", i)] = x2r
                 nc.sync.dma_start(out=x1raw[:, i, :, :], in_=x1_v[:, i, :, :])
-            if 13 <= i < 17:
-                load_x2n(i - 13)
+            if 4 <= i < 8:
+                a = 4 * (i - 4)
+                nc.sync.dma_start(out=x2n[:, a:a + 4, :], in_=x2n_v[:, a:a + 4, :])
             if i == 0:
                 nc.vector.tensor_tensor(out=kc[:], in0=c_bf[:], in1=c_bf[:], op=ALU.mult)
                 nc.vector.tensor_scalar_mul(out=kc[:], in0=kc[:], scalar1=-5.0 / 6.0 * SQRT5)
+            if i + 1 < NB:
+                stage_a(i + 1)
+            if 0 <= i - 1 < NB:
+                stage_cs(i - 1)
+            if 0 <= i < NB:
+                stage_b(i)
+            if 0 <= i - 1 < NB:
+                stage_d(i - 1)
+                stage_t(i - 1)
+            new_h = []
+            if 0 <= i - 2 < NB:
+                stage_qm(i - 2)
+                g, mc = ORDER[i - 2]
+                if g == 3:
+                    burst_m(mc)
+                    new_h.append((h_m, mc))
+            if 0 <= i - 3 < NB:
+                stage_qp(i - 3)
+                g, mc = ORDER[i - 3]
+                if mc == 3:
+                    burst_p(g)
+                    new_h.append((h_p, g))
             if i == 3:
                 nc.vector.tensor_tensor(out=k4[:], in0=l_bf[:], in1=l_bf[:], op=ALU.mult)
                 nc.vector.reciprocal(out=k4[:], in_=k4[:])
@@ -259,50 +275,22 @@ def tile_matern52_v_kernel(tc, X1, X2, c, l, r, grad_out, out_0, out_1):
                 for f in range(4):
                     nc.tensor.matmul(out=kp[:, f * P:(f + 1) * P], lhsT=k4[:, f:f + 1].to_broadcast([P, P]),
                                      rhs=ident[:], start=True, stop=True)
-            tb = i - 1
-            has_t = 0 <= tb < NB
-            if has_t:
-                stage_d(tb, 0)
-                stage_d(tb, 1)
-                for q in range(4):
-                    stage_cs(tb, q)
             if 0 <= i - 2 < NB:
-                stage_q(i - 2)
-            if 0 <= i < NB:
-                stage_b(i)
-            if i + 1 < NB:
-                stage_a(i + 1, 0)
-                stage_a(i + 1, 1)
-            if has_t:
-                stage_t(tb, 0)
-                stage_t(tb, 1)
-                stage_cs_out(tb)
+                stage_e(i - 2)
+            if 0 <= i - 1 < NB:
+                stage_r(i - 1)
+            if i == 3:
+                nc.scalar.copy(out=ktile[:], in_=kp[:])
             if 0 <= i < NB:
                 stage_c(i)
-            if has_t:
-                stage_e(tb, 0)
-                stage_e(tb, 1)
-            if i == 3:
-                nc.vector.tensor_copy(out=ktile[:], in_=kp[:])
             if 1 <= i < 5:
-                st[("x2g", i - 1)] = x_group(st[("x2r", i - 1)][:], 0)
+                st[("x2g", i - 1)] = x_group(st[("x2r", i - 1)][:], True)
             if 2 <= i < 6:
                 x_quant(st[("x2g", i - 2)], x2c[:, i - 2, :], x2s[:, i - 2, :])
-            if 10 <= i < 14:
-                st[("x1g", i - 10)] = x_group(x1raw[:, i - 10, :, :], 1)
-            if 11 <= i < 15:
-                x_quant(st[("x1g", i - 11)], x1c[:, i - 11, :], x1s[:, i - 11, :])
-            pb = i - 3
-            if 0 <= pb < NB and pb % 4 == 3:
-                h_p(pb // 4)
-            if 12 <= pb < NB:
-                h_m(pb - 12)
-            if 0 <= pb < NB and pb % 4 == 3:
-                store_p(pb // 4)
-            if 12 <= pb < NB:
-                store_m(pb - 12)
-            qb = i - 2
-            if 0 <= qb < NB and qb % 4 == 3:
-                burst_p(qb // 4)
-            if 12 <= qb < NB:
-                burst_m(qb - 12)
+            if 5 <= i < 9:
+                st[("x1g", i - 5)] = x_group(x1raw[:, i - 5, :, :], i - 5 < X1_ON_VECTOR)
+            if 6 <= i < 10:
+                x_quant(st[("x1g", i - 6)], x1c[:, i - 6, :], x1s[:, i - 6, :])
+            for fn, arg in pend_h:
+                fn(arg)
+            pend_h = new_h

from contextlib import ExitStack
import math

import concourse.mybir as mybir
from concourse.masks import make_identity

N1, N2, D = 2048, 2048, 512
FLOPS = 2 * 2 * N1 * N2 * D

F32 = mybir.dt.float32
BF16 = mybir.dt.bfloat16
U32 = mybir.dt.uint32
U8 = mybir.dt.uint8
E4 = mybir.dt.float8_e4m3fn_x4
E5 = mybir.dt.float8_e5m2_x4
ALU = mybir.AluOpType
ACT = mybir.ActivationFunctionType
AX = mybir.AxisListType

P = 128
SQRT5 = math.sqrt(5.0)
NB = 16
R_ON_VECTOR = 0
X1_ON_VECTOR = 2


def tile_matern52_v_kernel(tc, X1, X2, c, l, r, grad_out, out_0, out_1):
    nc = tc.nc
    ORDER = [(g, mc) for g in range(2) for mc in range(4)] + [(g, mc) for mc in range(4) for g in (2, 3)]
    r_v = r.rearrange("(g p j) m -> p g j m", g=4, j=4)
    go_v = grad_out.rearrange("(g p j) m -> p g j m", g=4, j=4)
    x1_v = X1.rearrange("(g p j) d -> p g j d", g=4, j=4)
    x2_v = X2.rearrange("(g p j) d -> p g j d", g=4, j=4)
    x2n_v = X2.rearrange("(a p) d -> p a d", p=P)
    o0_v = out_0.rearrange("(g p j) d -> p g j d", g=4, j=4)

    with ExitStack() as ctx:
        keep = ctx.enter_context(tc.tile_pool(name="keep", bufs=1))
        work = ctx.enter_context(tc.tile_pool(name="work", bufs=2))
        psum = ctx.enter_context(tc.psum_pool(name="psum", bufs=1))
        ctx.enter_context(tc.manual_schedule())

        c_bf = keep.tile([P, 1], BF16, name="c_bf")
        nc.scalar.dma_start(out=c_bf[:], in_=c.partition_broadcast(P))
        warm = keep.tile([P, 1], F32, name="warm")
        nc.vector.memset(warm[:], 0.0)
        nc.scalar.activation(out=warm[:], in_=warm[:], func=ACT.Exp)
        l_bf = keep.tile([P, 4], BF16, name="l_bf")
        with nc.allow_non_contiguous_dma(reason="512 lengthscales, one element a piece, once"):
            nc.gpsimd.dma_start(out=l_bf[:], in_=l.rearrange("(f p) -> p f", p=P))
        ident = keep.tile([P, P], F32, name="ident")
        make_identity(nc, ident[:])
        junk = keep.tile([P, P], BF16, name="junk")

        x1raw = keep.tile([P, 4, 4, D], BF16, name="x1raw")
        x2n = keep.tile([P, 16, D], BF16, name="x2n")
        x1c = keep.tile([P, 4, D], U32, name="x1c", align_bytes=64)
        x1s = keep.tile([P, 4, D], U8, name="x1s", align_bytes=64)
        x2c = keep.tile([P, 4, D], U32, name="x2c", align_bytes=64)
        x2s = keep.tile([P, 4, D], U8, name="x2s", align_bytes=64)
        cM = keep.tile([P, 4, N2], U32, name="cM", align_bytes=64)
        sM = keep.tile([P, 4, N2], U8, name="sM", align_bytes=64)
        rs_part = keep.tile([P, 16, 4], F32, name="rs_part")
        rs = keep.tile([P, 16], F32, name="rs")
        cs_part = keep.tile([P, 4, 16], F32, name="cs_part")
        cs = keep.tile([P, 16], F32, name="cs")
        kc = keep.tile([P, 1], F32, name="kc")
        k4 = keep.tile([P, 4], F32, name="k4")
        ktile = keep.tile([P, D], F32, name="ktile")

        st = {}

        def load(b):
            g, mc = ORDER[b]
            cols = (mc * 512, (mc + 1) * 512)
            rt = work.tile([P, 4, 512], F32, name="rt", tag="rt", bufs=3)
            if b == 0:
                for h in range(2):
                    nc.sync.dma_start(out=rt[:, 2 * h:2 * h + 2, :], in_=r_v[:, g, 2 * h:2 * h + 2, 0:512])
            else:
                nc.sync.dma_start(out=rt[:], in_=r_v[:, g, :, cols[0]:cols[1]])
            gt = work.tile([P, 4, 512], BF16, name="gt", tag="gt", bufs=3)
            nc.sync.dma_start(out=gt[:], in_=go_v[:, g, :, cols[0]:cols[1]])
            st[("rt", b)] = rt
            st[("gt", b)] = gt

        def stage_a(b):
            G = work.tile([P, 4, 512], F32, name="gblk", tag="gblk", bufs=3)
            st[("G", b)] = G
            rt = st[("rt", b)]
            if b == 0:
                for h in range(2):
                    nc.scalar.activation(out=G[:, 2 * h:2 * h + 2, :], in_=rt[:, 2 * h:2 * h + 2, :],
                                         func=ACT.Exp, scale=-SQRT5)
            else:
                nc.scalar.activation(out=G[:], in_=rt[:], func=ACT.Exp, scale=-SQRT5)

        def stage_b(b):
            G = st[("G", b)]
            nc.vector.scalar_tensor_tensor(out=G[:], in0=st[("rt", b)][:], scalar=1.0 / SQRT5, in1=G[:],
                                           op0=ALU.add, op1=ALU.mult)

        def stage_c(b):
            g, mc = ORDER[b]
            G = st[("G", b)]
            gt = st[("gt", b)]
            for j in range(4):
                nc.vector.scalar_tensor_tensor(out=G[:, j, :], in0=G[:, j, :], scalar=kc[:, 0:1],
                                               in1=gt[:, j, :], op0=ALU.mult, op1=ALU.mult,
                                               accum_out=rs_part[:, 4 * g + j, mc:mc + 1])

        def stage_d(b):
            tm = work.tile([P, 512, 4], BF16, name="tm", tag="tm", bufs=3, align_bytes=64)
            st[("tm", b)] = tm
            nc.scalar.copy(out=tm[:].rearrange("p (a i) t -> p a t i", i=4),
                           in_=st[("G", b)][:].rearrange("p t (a i) -> p a t i", i=4))

        def stage_cs(b):
            G = st[("G", b)]
            csp = psum.tile([P, 4, P], F32, name="csp", tag="csp", bufs=1)
            st[("csp", b)] = csp
            for q in range(4):
                for j in range(4):
                    nc.tensor.matmul(out=csp[:, q, :], lhsT=G[:, j, q * P:(q + 1) * P], rhs=ident[:],
                                     is_transpose=True, start=(j == 0), stop=(j == 3))

        def stage_r(b):
            g, mc = ORDER[b]
            csp = st[("csp", b)]
            if b < R_ON_VECTOR:
                nc.vector.tensor_reduce(out=cs_part[:, g, 4 * mc:4 * mc + 4], in_=csp[:], axis=AX.X, op=ALU.add)
            for q in range(4 if b >= R_ON_VECTOR else 0):
                nc.scalar.activation(out=junk[:], in_=csp[:, q, :], func=ACT.Copy,
                                     accum_out=cs_part[:, g, 4 * mc + q:4 * mc + q + 1])

        def stage_t(b):
            tmw = st[("tm", b)][:].rearrange("p c t -> p (c t)").bitcast(F32)
            for u in range(2):
                pt = psum.tile([P, 4, P], F32, name="pt", tag="pt", bufs=3)
                for t in range(4):
                    nc.tensor.transpose(pt[:, t, :], tmw[:, 2 * t + u:1024:8], ident[:])
                st[("pt", b, u)] = pt

        def stage_e(b):
            fm = work.tile([P, 4, P, 4], BF16, name="fm", tag="fm", bufs=2, align_bytes=64)
            st[("fm", b)] = fm
            for u in range(2):
                src = st[("pt", b, u)][:].rearrange("q t p -> q (t p)").bitcast(BF16)
                nc.scalar.copy(out=fm[:, 2 * u:2 * u + 2, :, :],
                               in_=src.rearrange("q (t p e) -> q e p t", t=4, e=2))

        def stage_qm(b):
            g, mc = ORDER[b]
            nc.vector.quantize_mx(out=cM[:, g, mc * 512:(mc + 1) * 512].bitcast(E5),
                                  scales=sM[:, g, mc * 512:(mc + 1) * 512],
                                  in_=st[("tm", b)][:].rearrange("p c t -> p (c t)"))

        def stage_qp(b):
            g, mc = ORDER[b]
            if mc == 0:
                st[("cP", g)] = work.tile([P, 4, 512], U32, name="cP", tag="cP", bufs=2, align_bytes=64)
                st[("sP", g)] = work.tile([P, 4, 512], U8, name="sP", tag="sP", bufs=2, align_bytes=64)
            nc.vector.quantize_mx(out=st[("cP", g)][:, mc, :].bitcast(E5), scales=st[("sP", g)][:, mc, :],
                                  in_=st[("fm", b)][:].rearrange("p j n t -> p (j n t)"))

        def burst_p(g):
            cP = st[("cP", g)]
            sP = st[("sP", g)]
            for j in range(4):
                acc = psum.tile([P, D], F32, name="acc", tag="acc", bufs=4)
                for mc in range(4):
                    nc.tensor.matmul_mx(out=acc[:], lhsT=cP[:, mc, j * P:(j + 1) * P].bitcast(E5),
                                        lhsT_scale=sP[:, mc, j * P:(j + 1) * P],
                                        rhs=x2c[:, mc, :].bitcast(E4), rhs_scale=x2s[:, mc, :],
                                        start=(mc == 0), stop=(mc == 3))
                st[("accP", g, j)] = acc

        def burst_m(mc):
            for q in range(4):
                lo = mc * 512 + q * P
                acc = psum.tile([P, D], F32, name="acc", tag="acc", bufs=4)
                for g in range(4):
                    nc.tensor.matmul_mx(out=acc[:], lhsT=cM[:, g, lo:lo + P].bitcast(E5),
                                        lhsT_scale=sM[:, g, lo:lo + P],
                                        rhs=x1c[:, g, :].bitcast(E4), rhs_scale=x1s[:, g, :],
                                        start=(g == 0), stop=(g == 3))
                st[("accM", mc, q)] = acc

        def epilogue(items):
            zs = []
            for x_ap, s_ap, acc, dst in items:
                z = work.tile([P, D], F32, name="z", tag="z", bufs=4)
                nc.vector.scalar_tensor_tensor(out=z[:], in0=x_ap, scalar=s_ap, in1=acc[:],
                                               op0=ALU.mult, op1=ALU.subtract)
                zs.append(z)
            for i in (0, 2, 1, 3):
                o = work.tile([P, D], F32, name="o", tag="o", bufs=4)
                if i < 2:
                    nc.gpsimd.tensor_tensor(out=o[:], in0=zs[i][:], in1=ktile[:], op=ALU.mult)
                else:
                    nc.vector.tensor_tensor(out=o[:], in0=zs[i][:], in1=ktile[:], op=ALU.mult)
                nc.sync.dma_start(out=items[i][3], in_=o[:])

        def h_p(g):
            nc.vector.tensor_reduce(out=rs[:, 4 * g:4 * g + 4], in_=rs_part[:, 4 * g:4 * g + 4, :],
                                    axis=AX.X, op=ALU.add)
            epilogue([(x1raw[:, g, j, :], rs[:, 4 * g + j:4 * g + j + 1], st[("accP", g, j)], o0_v[:, g, j, :])
                      for j in range(4)])

        def h_m(mc):
            nc.vector.tensor_reduce(out=cs[:, 4 * mc:4 * mc + 4],
                                    in_=cs_part[:, :, 4 * mc:4 * mc + 4].rearrange("p g q -> p q g"),
                                    axis=AX.X, op=ALU.add)
            epilogue([(x2n[:, 4 * mc + q, :], cs[:, 4 * mc + q:4 * mc + q + 1], st[("accM", mc, q)],
                       out_1[(4 * mc + q) * P:(4 * mc + q + 1) * P, :]) for q in range(4)])

        def x_group(src, on_vector):
            xg = work.tile([P, D, 4], BF16, name="xg", tag="xg", bufs=2, align_bytes=64)
            dst_v = xg[:].rearrange("p (a i) j -> p a j i", i=4)
            src_v = src.rearrange("p j (a i) -> p a j i", i=4)
            if on_vector:
                nc.vector.tensor_copy(out=dst_v, in_=src_v)
            else:
                nc.scalar.copy(out=dst_v, in_=src_v)
            return xg

        def x_quant(xg, codes, scales):
            nc.vector.quantize_mx(out=codes.bitcast(E4), scales=scales,
                                  in_=xg[:].rearrange("p d j -> p (d j)"))

        pend_h = []
        for i in range(-1, NB + 4):
            if i == -1:
                load(0)
            if i + 2 < NB:
                load(i + 2)
            if 0 <= i < 4:
                x2r = work.tile([P, 4, D], BF16, name="x2r", tag="x2r", bufs=2)
                nc.sync.dma_start(out=x2r[:], in_=x2_v[:, i, :, :])
                st[("x2r", i)] = x2r
                nc.sync.dma_start(out=x1raw[:, i, :, :], in_=x1_v[:, i, :, :])
            if 4 <= i < 8:
                a = 4 * (i - 4)
                nc.sync.dma_start(out=x2n[:, a:a + 4, :], in_=x2n_v[:, a:a + 4, :])
            if i == 0:
                nc.vector.tensor_tensor(out=kc[:], in0=c_bf[:], in1=c_bf[:], op=ALU.mult)
                nc.vector.tensor_scalar_mul(out=kc[:], in0=kc[:], scalar1=-5.0 / 6.0 * SQRT5)
            if i + 1 < NB:
                stage_a(i + 1)
            if 0 <= i - 1 < NB:
                stage_cs(i - 1)
            if 0 <= i < NB:
                stage_b(i)
            if 0 <= i - 1 < NB:
                stage_d(i - 1)
                stage_t(i - 1)
            new_h = []
            if 0 <= i - 2 < NB:
                stage_qm(i - 2)
                g, mc = ORDER[i - 2]
                if g == 3:
                    burst_m(mc)
                    new_h.append((h_m, mc))
            if 0 <= i - 3 < NB:
                stage_qp(i - 3)
                g, mc = ORDER[i - 3]
                if mc == 3:
                    burst_p(g)
                    new_h.append((h_p, g))
            if i == 3:
                nc.vector.tensor_tensor(out=k4[:], in0=l_bf[:], in1=l_bf[:], op=ALU.mult)
                nc.vector.reciprocal(out=k4[:], in_=k4[:])
                nc.vector.tensor_scalar_mul(out=k4[:], in0=k4[:], scalar1=2.0)
                kp = psum.tile([P, D], F32, name="acc", tag="acc", bufs=4)
                for f in range(4):
                    nc.tensor.matmul(out=kp[:, f * P:(f + 1) * P], lhsT=k4[:, f:f + 1].to_broadcast([P, P]),
                                     rhs=ident[:], start=True, stop=True)
            if 0 <= i - 2 < NB:
                stage_e(i - 2)
            if 0 <= i - 1 < NB:
                stage_r(i - 1)
            if i == 3:
                nc.scalar.copy(out=ktile[:], in_=kp[:])
            if 0 <= i < NB:
                stage_c(i)
            if 1 <= i < 5:
                st[("x2g", i - 1)] = x_group(st[("x2r", i - 1)][:], True)
            if 2 <= i < 6:
                x_quant(st[("x2g", i - 2)], x2c[:, i - 2, :], x2s[:, i - 2, :])
            if 5 <= i < 9:
                st[("x1g", i - 5)] = x_group(x1raw[:, i - 5, :, :], i - 5 < X1_ON_VECTOR)
            if 6 <= i < 10:
                x_quant(st[("x1g", i - 6)], x1c[:, i - 6, :], x1s[:, i - 6, :])
            for fn, arg in pend_h:
                fn(arg)
            pend_h = new_h
